import numpy as np
import ml_dtypes


def mxq(x, axis, fmt="e4m3"):
    dtype, down = {"e4m3": (ml_dtypes.float8_e4m3fn, 7), "e5m2": (ml_dtypes.float8_e5m2, 14)}[fmt]
    v = np.moveaxis(np.asarray(x, np.float32).astype(ml_dtypes.bfloat16).astype(np.float64), axis, -1)
    blocks = v.reshape(v.shape[:-1] + (-1, 32))
    amax = np.abs(blocks).max(-1, keepdims=True)
    byte = np.maximum(np.where(amax > 0, np.frexp(amax)[1] - 1 + 127, 0) - down, 1)
    scale = np.exp2(byte - 127.0)
    codes = (blocks / scale).astype(np.float32).astype(dtype).astype(np.float64)
    return np.moveaxis((codes * scale).reshape(v.shape), -1, axis)


WIDE = False


def mx_kscale(k):
    if not WIDE:
        return np.ones(k)
    levels = np.array([10, -10, 5, -5, 0])
    if k % 512:
        return np.exp2(np.random.permutation(np.resize(levels, k // 32))).repeat(32)
    a = np.empty((k // 512, 16))
    for p in range(k // 512):
        a[p, :8] = np.random.permutation(np.resize(levels, 8))
        for g in range(8):
            far = levels[np.abs(levels - a[p, g]) >= 10]
            a[p, g + 8] = far[np.random.randint(len(far))]
    return np.exp2(a.ravel()).repeat(32)


BF16 = ml_dtypes.bfloat16


def bf(x):
    return np.asarray(x, np.float32).astype(BF16)


def f64(x):
    return np.asarray(x).astype(np.float64)


B, N, SR, SI, NH, NV, NC, NLON, NLAT = 2, 8, 1, 128, 4, 4, 32, 8, 8
S = SI * NH
MIN_SIGMA = 1e-10


def setup_inputs():
    s = mx_kscale(S)
    d = np.log2(s.max() / s)
    x0 = np.random.standard_normal((B, N, SR, S, NV, NC)) * 0.2 * np.sqrt(S)
    lon0 = np.random.standard_normal((B, N, SR, SI, NH))
    lat0 = np.random.standard_normal((B, N, SR, SI, NH))
    mus_lon = bf(np.linspace(-1.0, 1.0, NLON) + 0.03 * np.random.standard_normal(NLON))
    mus_lat = bf(np.linspace(-1.0, 1.0, NLAT) + 0.03 * np.random.standard_normal(NLAT))
    sigma = bf(0.4 + 0.2 * np.random.random(1))
    if d.max() > 0:
        sig = float(f64(sigma)[0])
        m0 = float(f64(mus_lon).min())
        lon0 = m0 - np.sqrt((0.3 * sig * lon0) ** 2 + 2.0 * np.log(2.0) * sig ** 2 * d.reshape(SI, NH))
    return {"x": bf(x0 * (2.0 ** d)[:, None, None]),
            "coords_lon": bf(lon0),
            "coords_lat": bf(lat0),
            "mus_lon": mus_lon,
            "mus_lat": mus_lat,
            "sigma": sigma}


def reference(x, coords_lon, coords_lat, mus_lon, mus_lat, sigma):
    x, coords_lon, coords_lat = f64(x), f64(coords_lon), f64(coords_lat)
    mus_lon, mus_lat, sigma = f64(mus_lon), f64(mus_lat), f64(sigma)
    b, n, sr, si, nh = coords_lon.shape
    nv, nc = x.shape[-2:]
    nlon, nlat = mus_lon.shape[0], mus_lat.shape[0]
    sig = np.maximum(sigma, MIN_SIGMA)
    wlon = np.exp(-0.5 * ((coords_lon[..., None] - mus_lon) / sig) ** 2)
    wlat = np.exp(-0.5 * ((coords_lat[..., None] - mus_lat) / sig) ** 2)
    w = (wlon[..., :, None] * wlat[..., None, :]).reshape(b, n, sr, si * nh, nlon, nlat)
    w = w / np.sum(w, axis=3, keepdims=True)
    wq = mxq(w, 3, "e4m3").reshape(b, n, sr, si * nh, nlon * nlat)
    xq = mxq(x, 3, "e4m3").reshape(b, n, sr, si * nh, nv * nc)
    out = xq.transpose(0, 1, 2, 4, 3) @ wq
    out = out.reshape(b, n, sr, nv, nc, nlon, nlat).transpose(0, 1, 2, 3, 5, 6, 4)
    return out.reshape(b, n * sr, nv, nlon, nlat, nc)

@@ -1,0 +1,258 @@
+from contextlib import ExitStack
+
+import concourse.mybir as mybir
+from concourse.masks import make_identity
+
+F32 = mybir.dt.float32
+BF16 = mybir.dt.bfloat16
+U32 = mybir.dt.uint32
+U8 = mybir.dt.uint8
+FP8X4 = mybir.dt.float8_e4m3fn_x4
+ACT = mybir.ActivationFunctionType
+ALU = mybir.AluOpType
+
+P = 128
+PACK = 4
+BATCH = 2
+PER_BATCH = 8
+OFFSETS = 8
+W_COLS = OFFSETS * OFFSETS
+X_COLS = 128
+C_LAST = 32
+PAIRS = 2
+CHUNKS = PER_BATCH // PAIRS
+UNITS = PACK * PAIRS
+BANK = 512
+SPREAD = PAIRS * P
+ROWS = PER_BATCH * 2 * BATCH
+POOL_CHUNKS = 2
+MIN_SIGMA = 1e-10
+
+FLOPS = 2 * BATCH * PER_BATCH * P * PACK * X_COLS * W_COLS
+
+
+def tile_normal_nolayer_s_kernel(
+    tc, x, coords_lon, coords_lat, mus_lon, mus_lat, sigma, out
+):
+    nc = tc.nc
+    with ExitStack() as ctx:
+        keep = ctx.enter_context(tc.tile_pool(name="keep", bufs=1))
+        ps_coords = ctx.enter_context(tc.psum_pool(name="ps_coords", bufs=1))
+        ps_norm = ctx.enter_context(tc.psum_pool(name="ps_norm", bufs=CHUNKS))
+        ps_out = ctx.enter_context(tc.psum_pool(name="ps_out", bufs=3))
+        ctx.enter_context(tc.manual_schedule())
+
+        coords = keep.tile([P, P * PACK], BF16)
+        mus = keep.tile([P, 2, 16], BF16)
+        mus_rows = keep.tile([P, PAIRS, 2, BATCH, OFFSETS], BF16)
+        offsets = keep.tile([P, CHUNKS, UNITS * 2 * BATCH, OFFSETS], F32)
+        sigma_bf = keep.tile([P, 1], BF16)
+        x_rows = keep.tile([P, CHUNKS, BATCH, PAIRS, PACK, X_COLS], BF16)
+        ident_bf = keep.tile([P, P], BF16)
+        ident_f32 = keep.tile([P, P], F32)
+        ones = keep.tile([P, 1], F32)
+        table_warm = keep.tile([P, 1], F32)
+        sigma_f32 = keep.tile([P, 1], F32)
+        inv_sigma = keep.tile([P, 1], F32)
+        gauss = keep.tile([P, CHUNKS, 2, UNITS * BATCH, OFFSETS], F32)
+        g = keep.tile([P, CHUNKS, UNITS, BATCH * W_COLS], F32)
+        g_sums = keep.tile([P, CHUNKS, PAIRS], F32)
+        inv_sums = keep.tile([P, CHUNKS, PAIRS], F32)
+        x_grouped = keep.tile([P, CHUNKS, PAIRS, BATCH, X_COLS, PACK], BF16, align_bytes=64)
+        x_codes = keep.tile([P, CHUNKS, PAIRS * BATCH * X_COLS], U32, align_bytes=64)
+        x_scales = keep.tile([P, CHUNKS, PAIRS * BATCH * X_COLS], U8, align_bytes=64)
+        w_bf = keep.tile([P, CHUNKS, PAIRS, P, PACK], BF16, align_bytes=64)
+        w_codes = keep.tile([P, CHUNKS, PAIRS * P], U32, align_bytes=64)
+        w_scales = keep.tile([P, CHUNKS, PAIRS * P], U8, align_bytes=64)
+        result = keep.tile([P, CHUNKS, PAIRS, X_COLS], F32)
+        coords_t = ps_coords.tile([P, PACK, P], BF16)
+        norms = [ps_norm.tile([P, BANK], F32, name="norm") for c in range(CHUNKS)]
+
+        for w, coords_w in enumerate((coords_lon, coords_lat)):
+            for a in range(BATCH):
+                nc.sync.dma_start(
+                    out=coords[w * BATCH + a : ROWS : 2 * BATCH, :],
+                    in_=coords_w[a].rearrange("j o i h -> (j o) (i h)"),
+                )
+        nc.scalar.dma_start(out=mus[:, 0, 0:OFFSETS], in_=mus_lon.partition_broadcast(P))
+        nc.scalar.dma_start(out=mus[:, 1, 0:OFFSETS], in_=mus_lat.partition_broadcast(P))
+        nc.scalar.dma_start(out=sigma_bf[:], in_=sigma.partition_broadcast(P))
+        for c in range(CHUNKS):
+            for a in range(BATCH):
+                nc.sync.dma_start(
+                    out=x_rows[:, c, a].rearrange("p j t n -> p j (t n)"),
+                    in_=x[a, c * PAIRS : (c + 1) * PAIRS, 0].rearrange(
+                        "j (p t) v k -> p j (t v k)", t=PACK
+                    ),
+                )
+
+        nc.vector.memset(coords[ROWS:64, :], 0.0)
+        nc.vector.memset(coords[64:P, :], 0.0)
+        make_identity(nc, ident_bf[:])
+        make_identity(nc, ident_f32[:])
+        nc.vector.memset(ones[:], 1.0)
+        nc.scalar.activation(out=table_warm[:], in_=ones[:], func=ACT.Exp)
+        nc.vector.tensor_scalar_max(out=sigma_f32[:], in0=sigma_bf[:], scalar1=MIN_SIGMA)
+        nc.vector.reciprocal(out=inv_sigma[:], in_=sigma_f32[:])
+
+        for w in range(2):
+            nc.vector.tensor_copy(
+                out=mus_rows[:, :, w],
+                in_=mus[:, w, 0:OFFSETS]
+                .unsqueeze(1)
+                .unsqueeze(1)
+                .to_broadcast([P, PAIRS, BATCH, OFFSETS]),
+            )
+
+        for t in range(PACK):
+            nc.tensor.transpose(
+                out=coords_t[:, t], in_=coords[:, t::PACK], identity=ident_bf[:]
+            )
+
+        def gaussians(c):
+            rows = PAIRS * 2 * BATCH
+            shape = [P, PACK, rows, OFFSETS]
+            nc.vector.tensor_tensor(
+                out=offsets[:, c].rearrange("p (t r) m -> p t r m", t=PACK),
+                in0=coords_t[:, :, c * rows : (c + 1) * rows].unsqueeze(3).to_broadcast(shape),
+                in1=mus_rows[:]
+                .rearrange("p j w a m -> p (j w a) m")
+                .unsqueeze(1)
+                .to_broadcast(shape),
+                op=ALU.subtract,
+            )
+            nc.scalar.activation(
+                out=gauss[:, c].rearrange("p w (u a) m -> p u w (a m)", a=BATCH),
+                in_=offsets[:, c].rearrange("p (u w a) m -> p u w (a m)", w=2, a=BATCH),
+                func=ACT.Square,
+                scale=inv_sigma[:, 0:1],
+            )
+            flat = gauss[:, c].rearrange("p w e m -> p (w e m)")
+            nc.scalar.activation(out=flat, in_=flat, func=ACT.Exp, scale=-0.5)
+
+        def products(c):
+            shape = [P, UNITS * BATCH, OFFSETS, OFFSETS]
+            engine = nc.vector if c < CHUNKS - POOL_CHUNKS else nc.gpsimd
+            engine.tensor_tensor(
+                out=g[:, c].rearrange("p u (a m n) -> p (u a) m n", a=BATCH, m=OFFSETS),
+                in0=gauss[:, c, 0].unsqueeze(3).to_broadcast(shape),
+                in1=gauss[:, c, 1].unsqueeze(2).to_broadcast(shape),
+                op=ALU.mult,
+            )
+
+        def sums(c):
+            for j in range(PAIRS):
+                for t in range(PACK):
+                    nc.tensor.matmul(
+                        out=norms[c][:, j * P : (j + 1) * P],
+                        lhsT=g[:, c, t * PAIRS + j],
+                        rhs=ident_f32[:],
+                        is_transpose=True,
+                        start=(t == 0),
+                        stop=(t == PACK - 1),
+                    )
+
+        def invert(c):
+            nc.vector.tensor_reduce(
+                out=g_sums[:, c],
+                in_=norms[c][:, 0:SPREAD].rearrange("p (j i) -> p j i", j=PAIRS),
+                axis=mybir.AxisListType.X,
+                op=ALU.add,
+            )
+            nc.vector.reciprocal(out=inv_sums[:, c], in_=g_sums[:, c])
+
+        def spread(c):
+            for j in range(PAIRS):
+                nc.tensor.transpose(
+                    out=norms[c][:, SPREAD + j * P : SPREAD + (j + 1) * P],
+                    in_=inv_sums[:, c, j : j + 1].to_broadcast([P, P]),
+                    identity=ident_f32[:],
+                )
+
+        def regroup_x(c):
+            for j in range(PAIRS):
+                for a in range(BATCH):
+                    nc.scalar.copy(
+                        out=x_grouped[:, c, j, a].rearrange("p (n i) t -> p n t i", i=4),
+                        in_=x_rows[:, c, a, j].rearrange("p t (n i) -> p n t i", i=4),
+                    )
+
+        def quantise_x(c):
+            nc.vector.quantize_mx(
+                out=x_codes[:, c].bitcast(FP8X4),
+                scales=x_scales[:, c],
+                in_=x_grouped[:, c].rearrange("p j a n t -> p (j a n t)"),
+            )
+
+        def normalise(c):
+            shape = [P, PAIRS, P, PACK]
+            nc.vector.tensor_tensor(
+                out=w_bf[:, c],
+                in0=g[:, c].rearrange("p (t j) n -> p j n t", t=PACK),
+                in1=norms[c][:, SPREAD : SPREAD + PAIRS * P]
+                .rearrange("p (j n) -> p j n", j=PAIRS)
+                .unsqueeze(3)
+                .to_broadcast(shape),
+                op=ALU.mult,
+            )
+
+        def quantise_w(c):
+            nc.vector.quantize_mx(
+                out=w_codes[:, c].bitcast(FP8X4),
+                scales=w_scales[:, c],
+                in_=w_bf[:, c].rearrange("p j n t -> p (j n t)"),
+            )
+
+        accs = {}
+
+        def multiply(c):
+            accs[c] = ps_out.tile([P, PAIRS, BATCH, X_COLS], F32, name="acc")
+            for j in range(PAIRS):
+                w_cols = slice(j * P, (j + 1) * P)
+                x_cols = slice(j * BATCH * X_COLS, (j + 1) * BATCH * X_COLS)
+                nc.tensor.matmul_mx(
+                    out=accs[c][:, j].rearrange("p a n -> p (a n)"),
+                    lhsT=w_codes[:, c, w_cols].bitcast(FP8X4),
+                    lhsT_scale=w_scales[:, c, w_cols],
+                    rhs=x_codes[:, c, x_cols].bitcast(FP8X4),
+                    rhs_scale=x_scales[:, c, x_cols],
+                    start=True,
+                    stop=True,
+                )
+
+        def store(c, first_half):
+            first_half(out=result[0:64, c], in_=accs[c][0:64, :, 0, :])
+            nc.scalar.copy(out=result[64:128, c], in_=accs[c][64:128, :, 1, :])
+            for a in range(BATCH):
+                nc.sync.dma_start(
+                    out=out[a, c * PAIRS : (c + 1) * PAIRS].rearrange(
+                        "j v m n k -> (m n) (j v) k"
+                    ),
+                    in_=result[a * 64 : (a + 1) * 64, c].rearrange(
+                        "p j (v k) -> p (j v) k", k=C_LAST
+                    ),
+                )
+
+        for c in range(CHUNKS):
+            gaussians(c)
+        for c in range(CHUNKS):
+            regroup_x(c)
+        for c in range(CHUNKS):
+            products(c)
+        sums(0)
+        invert(0)
+        spread(0)
+        sums(1)
+        for c in range(CHUNKS):
+            normalise(c)
+            if c + 1 < CHUNKS:
+                invert(c + 1)
+                spread(c + 1)
+            if c + 2 < CHUNKS:
+                sums(c + 2)
+            quantise_x(c)
+            quantise_w(c)
+            multiply(c)
+            if c >= 1:
+                store(c - 1, nc.scalar.copy)
+        store(CHUNKS - 1, nc.vector.tensor_copy)

@@ -13,22 +13,23 @@ ALU = mybir.AluOpType
 
 P = 128
 PACK = 4
-BATCH = 2
-PER_BATCH = 8
+WINDOWS = 16
 OFFSETS = 8
 W_COLS = OFFSETS * OFFSETS
 X_COLS = 128
 C_LAST = 32
-PAIRS = 2
-CHUNKS = PER_BATCH // PAIRS
-UNITS = PACK * PAIRS
-BANK = 512
-SPREAD = PAIRS * P
-ROWS = PER_BATCH * 2 * BATCH
-POOL_CHUNKS = 2
+CHUNK = 4
+CHUNKS = WINDOWS // CHUNK
+PAIRS = CHUNK // 2
+HALF = WINDOWS // 2
+N_HALF = OFFSETS // 2
+MM_WINDOWS = 12
+MM_ROWS = MM_WINDOWS * OFFSETS
+LAST = CHUNKS - 1
+V_WINDOWS = 2
 MIN_SIGMA = 1e-10
 
-FLOPS = 2 * BATCH * PER_BATCH * P * PACK * X_COLS * W_COLS
+FLOPS = 2 * WINDOWS * P * PACK * X_COLS * W_COLS
 
 
 def tile_normal_nolayer_s_kernel(
@@ -37,161 +38,234 @@ def tile_normal_nolayer_s_kernel(
     nc = tc.nc
     with ExitStack() as ctx:
         keep = ctx.enter_context(tc.tile_pool(name="keep", bufs=1))
-        ps_coords = ctx.enter_context(tc.psum_pool(name="ps_coords", bufs=1))
-        ps_norm = ctx.enter_context(tc.psum_pool(name="ps_norm", bufs=CHUNKS))
+        ps = ctx.enter_context(tc.psum_pool(name="ps", bufs=1))
         ps_out = ctx.enter_context(tc.psum_pool(name="ps_out", bufs=3))
         ctx.enter_context(tc.manual_schedule())
 
         coords = keep.tile([P, P * PACK], BF16)
         mus = keep.tile([P, 2, 16], BF16)
-        mus_rows = keep.tile([P, PAIRS, 2, BATCH, OFFSETS], BF16)
-        offsets = keep.tile([P, CHUNKS, UNITS * 2 * BATCH, OFFSETS], F32)
         sigma_bf = keep.tile([P, 1], BF16)
-        x_rows = keep.tile([P, CHUNKS, BATCH, PAIRS, PACK, X_COLS], BF16)
+        x_rows = keep.tile([P, WINDOWS, PACK, X_COLS], BF16)
         ident_bf = keep.tile([P, P], BF16)
         ident_f32 = keep.tile([P, P], F32)
+        same_window = keep.tile([P, MM_ROWS], F32)
         ones = keep.tile([P, 1], F32)
         table_warm = keep.tile([P, 1], F32)
         sigma_f32 = keep.tile([P, 1], F32)
         inv_sigma = keep.tile([P, 1], F32)
-        gauss = keep.tile([P, CHUNKS, 2, UNITS * BATCH, OFFSETS], F32)
-        g = keep.tile([P, CHUNKS, UNITS, BATCH * W_COLS], F32)
-        g_sums = keep.tile([P, CHUNKS, PAIRS], F32)
-        inv_sums = keep.tile([P, CHUNKS, PAIRS], F32)
-        x_grouped = keep.tile([P, CHUNKS, PAIRS, BATCH, X_COLS, PACK], BF16, align_bytes=64)
-        x_codes = keep.tile([P, CHUNKS, PAIRS * BATCH * X_COLS], U32, align_bytes=64)
-        x_scales = keep.tile([P, CHUNKS, PAIRS * BATCH * X_COLS], U8, align_bytes=64)
-        w_bf = keep.tile([P, CHUNKS, PAIRS, P, PACK], BF16, align_bytes=64)
-        w_codes = keep.tile([P, CHUNKS, PAIRS * P], U32, align_bytes=64)
-        w_scales = keep.tile([P, CHUNKS, PAIRS * P], U8, align_bytes=64)
+        exp_scale = keep.tile([P, 1], F32)
+        dist = keep.tile([P, PACK, 2, WINDOWS, OFFSETS], F32)
+        gauss = keep.tile([P, PACK, 2, WINDOWS, OFFSETS], F32)
+        g = keep.tile([P, PACK, WINDOWS, W_COLS], F32)
+        sums_masked = keep.tile([P, MM_WINDOWS, OFFSETS], F32)
+        g_sums = keep.tile([P, OFFSETS], F32)
+        inv_sums = keep.tile([P, OFFSETS], F32)
+        last_sums = keep.tile([P, PAIRS], F32)
+        inv_last = keep.tile([P, PAIRS], F32)
+        x_grouped = keep.tile([P, WINDOWS, X_COLS, PACK], BF16, align_bytes=64)
+        x_codes = keep.tile([P, CHUNKS, CHUNK * X_COLS], U32, align_bytes=64)
+        x_scales = keep.tile([P, CHUNKS, CHUNK * X_COLS], U8, align_bytes=64)
+        w_bf = keep.tile([P, CHUNKS, CHUNK * OFFSETS, OFFSETS, PACK], BF16, align_bytes=64)
+        w_codes = keep.tile([P, CHUNKS, CHUNK * W_COLS], U32, align_bytes=64)
+        w_scales = keep.tile([P, CHUNKS, CHUNK * W_COLS], U8, align_bytes=64)
         result = keep.tile([P, CHUNKS, PAIRS, X_COLS], F32)
-        coords_t = ps_coords.tile([P, PACK, P], BF16)
-        norms = [ps_norm.tile([P, BANK], F32, name="norm") for c in range(CHUNKS)]
+        coords_t = ps.tile([P, PACK, P], BF16, name="coords_t")
+        cross_sums = ps.tile([P, MM_ROWS], F32, name="cross_sums")
+        norm_last = ps.tile([P, 2, PAIRS, P], F32, name="norm_last")
+        norms = [ps.tile([P, N_HALF, P], F32, name="norm%d" % i) for i in range(2)]
 
         for w, coords_w in enumerate((coords_lon, coords_lat)):
-            for a in range(BATCH):
-                nc.sync.dma_start(
-                    out=coords[w * BATCH + a : ROWS : 2 * BATCH, :],
-                    in_=coords_w[a].rearrange("j o i h -> (j o) (i h)"),
-                )
+            nc.sync.dma_start(
+                out=coords[w * WINDOWS : (w + 1) * WINDOWS, :],
+                in_=coords_w.rearrange("a n o i h -> (a n o) (i h)"),
+            )
         nc.scalar.dma_start(out=mus[:, 0, 0:OFFSETS], in_=mus_lon.partition_broadcast(P))
-        nc.scalar.dma_start(out=mus[:, 1, 0:OFFSETS], in_=mus_lat.partition_broadcast(P))
+        nc.sync.dma_start(out=mus[:, 1, 0:OFFSETS], in_=mus_lat.partition_broadcast(P))
         nc.scalar.dma_start(out=sigma_bf[:], in_=sigma.partition_broadcast(P))
+        x_by_window = x.rearrange("a n o (p t) v k -> p (a n o) (t v k)", t=PACK)
         for c in range(CHUNKS):
-            for a in range(BATCH):
-                nc.sync.dma_start(
-                    out=x_rows[:, c, a].rearrange("p j t n -> p j (t n)"),
-                    in_=x[a, c * PAIRS : (c + 1) * PAIRS, 0].rearrange(
-                        "j (p t) v k -> p j (t v k)", t=PACK
-                    ),
-                )
+            windows = slice(c * CHUNK, (c + 1) * CHUNK)
+            nc.sync.dma_start(
+                out=x_rows[:, windows].rearrange("p w t n -> p w (t n)"),
+                in_=x_by_window[:, windows],
+            )
 
-        nc.vector.memset(coords[ROWS:64, :], 0.0)
+        nc.vector.memset(coords[2 * WINDOWS : 64, :], 0.0)
         nc.vector.memset(coords[64:P, :], 0.0)
+        nc.vector.memset(ones[:], 1.0)
+        nc.vector.memset(inv_sums[MM_ROWS:P, :], 1.0)
         make_identity(nc, ident_bf[:])
         make_identity(nc, ident_f32[:])
-        nc.vector.memset(ones[:], 1.0)
-        nc.scalar.activation(out=table_warm[:], in_=ones[:], func=ACT.Exp)
-        nc.vector.tensor_scalar_max(out=sigma_f32[:], in0=sigma_bf[:], scalar1=MIN_SIGMA)
-        nc.vector.reciprocal(out=inv_sigma[:], in_=sigma_f32[:])
-
-        for w in range(2):
-            nc.vector.tensor_copy(
-                out=mus_rows[:, :, w],
-                in_=mus[:, w, 0:OFFSETS]
-                .unsqueeze(1)
-                .unsqueeze(1)
-                .to_broadcast([P, PAIRS, BATCH, OFFSETS]),
+        nc.gpsimd.memset(same_window[:], 1.0)
+        for op, base, sign in ((ALU.is_ge, 0, 1), (ALU.is_gt, OFFSETS, -1)):
+            nc.gpsimd.affine_select(
+                out=same_window[:],
+                in_=same_window[:],
+                compare_op=op,
+                fill=0.0,
+                base=base,
+                pattern=[[-sign * OFFSETS, MM_WINDOWS], [0, OFFSETS]],
+                channel_multiplier=sign,
             )
+        nc.scalar.activation(out=table_warm[:], in_=ones[:], func=ACT.Exp)
 
         for t in range(PACK):
             nc.tensor.transpose(
                 out=coords_t[:, t], in_=coords[:, t::PACK], identity=ident_bf[:]
             )
 
-        def gaussians(c):
-            rows = PAIRS * 2 * BATCH
-            shape = [P, PACK, rows, OFFSETS]
+        def distances(t):
+            shape = [P, 2, WINDOWS, OFFSETS]
             nc.vector.tensor_tensor(
-                out=offsets[:, c].rearrange("p (t r) m -> p t r m", t=PACK),
-                in0=coords_t[:, :, c * rows : (c + 1) * rows].unsqueeze(3).to_broadcast(shape),
-                in1=mus_rows[:]
-                .rearrange("p j w a m -> p (j w a) m")
-                .unsqueeze(1)
+                out=dist[:, t],
+                in0=coords_t[:, t, 0 : 2 * WINDOWS]
+                .rearrange("p (d w) -> p d w", d=2)
+                .unsqueeze(3)
                 .to_broadcast(shape),
+                in1=mus[:, :, 0:OFFSETS].unsqueeze(2).to_broadcast(shape),
                 op=ALU.subtract,
             )
-            nc.scalar.activation(
-                out=gauss[:, c].rearrange("p w (u a) m -> p u w (a m)", a=BATCH),
-                in_=offsets[:, c].rearrange("p (u w a) m -> p u w (a m)", w=2, a=BATCH),
-                func=ACT.Square,
-                scale=inv_sigma[:, 0:1],
-            )
-            flat = gauss[:, c].rearrange("p w e m -> p (w e m)")
-            nc.scalar.activation(out=flat, in_=flat, func=ACT.Exp, scale=-0.5)
 
-        def products(c):
-            shape = [P, UNITS * BATCH, OFFSETS, OFFSETS]
-            engine = nc.vector if c < CHUNKS - POOL_CHUNKS else nc.gpsimd
+        def limit_sigma():
+            nc.vector.tensor_scalar_max(out=sigma_f32[:], in0=sigma_bf[:], scalar1=MIN_SIGMA)
+
+        def invert_sigma():
+            nc.vector.reciprocal(out=inv_sigma[:], in_=sigma_f32[:])
+
+        def find_exp_scale():
+            nc.vector.scalar_tensor_tensor(
+                out=exp_scale[:],
+                in0=inv_sigma[:],
+                scalar=-0.5,
+                in1=inv_sigma[:],
+                op0=ALU.mult,
+                op1=ALU.mult,
+            )
+
+        def square(t):
+            flat = dist[:, t].rearrange("p d w m -> p (d w m)")
+            if t == 0:
+                nc.scalar.activation(out=flat, in_=flat, func=ACT.Square)
+            else:
+                nc.vector.tensor_tensor(out=flat, in0=flat, in1=flat, op=ALU.mult)
+
+        def gaussians(t):
+            nc.scalar.activation(
+                out=gauss[:, t].rearrange("p d w m -> p (d w m)"),
+                in_=dist[:, t].rearrange("p d w m -> p (d w m)"),
+                func=ACT.Exp,
+                scale=exp_scale[:, 0:1],
+            )
+
+        def products(engine, half, t):
+            windows = slice(half * HALF, (half + 1) * HALF)
+            shape = [P, HALF, OFFSETS, OFFSETS]
             engine.tensor_tensor(
-                out=g[:, c].rearrange("p u (a m n) -> p (u a) m n", a=BATCH, m=OFFSETS),
-                in0=gauss[:, c, 0].unsqueeze(3).to_broadcast(shape),
-                in1=gauss[:, c, 1].unsqueeze(2).to_broadcast(shape),
+                out=g[:, t, windows].rearrange("p w (m n) -> p w m n", m=OFFSETS),
+                in0=gauss[:, t, 0, windows].unsqueeze(3).to_broadcast(shape),
+                in1=gauss[:, t, 1, windows].unsqueeze(2).to_broadcast(shape),
                 op=ALU.mult,
             )
 
-        def sums(c):
+        def sum_over_neighbours(t):
+            nc.tensor.matmul(
+                out=cross_sums[:],
+                lhsT=gauss[:, t, 0].rearrange("p w m -> p (w m)"),
+                rhs=gauss[:, t, 1, 0:MM_WINDOWS].rearrange("p w m -> p (w m)"),
+                start=(t == 0),
+                stop=(t == PACK - 1),
+            )
+
+        def mask_sums():
+            nc.vector.tensor_tensor(
+                out=sums_masked[0:MM_ROWS].rearrange("p w n -> p (w n)"),
+                in0=cross_sums[0:MM_ROWS],
+                in1=same_window[0:MM_ROWS],
+                op=ALU.mult,
+            )
+
+        def pick_sums():
+            nc.vector.tensor_reduce(
+                out=g_sums[0:MM_ROWS],
+                in_=sums_masked[0:MM_ROWS].rearrange("p w n -> p n w"),
+                axis=mybir.AxisListType.X,
+                op=ALU.add,
+            )
+
+        def invert_sums():
+            nc.vector.reciprocal(out=inv_sums[0:MM_ROWS], in_=g_sums[0:MM_ROWS])
+            for n in range(OFFSETS):
+                nc.tensor.transpose(
+                    out=norms[n // N_HALF][:, n % N_HALF],
+                    in_=inv_sums[:, n : n + 1].to_broadcast([P, P]),
+                    identity=ident_f32[:],
+                )
+
+        def sum_last():
             for j in range(PAIRS):
+                first = LAST * CHUNK + 2 * j
                 for t in range(PACK):
                     nc.tensor.matmul(
-                        out=norms[c][:, j * P : (j + 1) * P],
-                        lhsT=g[:, c, t * PAIRS + j],
+                        out=norm_last[:, 0, j],
+                        lhsT=g[:, t, first : first + 2].rearrange("p w k -> p (w k)"),
                         rhs=ident_f32[:],
                         is_transpose=True,
                         start=(t == 0),
                         stop=(t == PACK - 1),
                     )
 
-        def invert(c):
+        def pick_last():
             nc.vector.tensor_reduce(
-                out=g_sums[:, c],
-                in_=norms[c][:, 0:SPREAD].rearrange("p (j i) -> p j i", j=PAIRS),
+                out=last_sums[:],
+                in_=norm_last[:, 0],
                 axis=mybir.AxisListType.X,
                 op=ALU.add,
             )
-            nc.vector.reciprocal(out=inv_sums[:, c], in_=g_sums[:, c])
 
-        def spread(c):
+        def invert_last():
+            nc.vector.reciprocal(out=inv_last[:], in_=last_sums[:])
             for j in range(PAIRS):
                 nc.tensor.transpose(
-                    out=norms[c][:, SPREAD + j * P : SPREAD + (j + 1) * P],
-                    in_=inv_sums[:, c, j : j + 1].to_broadcast([P, P]),
+                    out=norm_last[:, 1, j],
+                    in_=inv_last[:, j : j + 1].to_broadcast([P, P]),
                     identity=ident_f32[:],
                 )
 
-        def regroup_x(c):
-            for j in range(PAIRS):
-                for a in range(BATCH):
-                    nc.scalar.copy(
-                        out=x_grouped[:, c, j, a].rearrange("p (n i) t -> p n t i", i=4),
-                        in_=x_rows[:, c, a, j].rearrange("p t (n i) -> p n t i", i=4),
-                    )
+        def regroup_x(copy, window):
+            copy(
+                out=x_grouped[:, window].rearrange("p (n i) t -> p n t i", i=4),
+                in_=x_rows[:, window].rearrange("p t (n i) -> p n t i", i=4),
+            )
 
         def quantise_x(c):
             nc.vector.quantize_mx(
                 out=x_codes[:, c].bitcast(FP8X4),
                 scales=x_scales[:, c],
-                in_=x_grouped[:, c].rearrange("p j a n t -> p (j a n t)"),
+                in_=x_grouped[:, c * CHUNK : (c + 1) * CHUNK].rearrange("p w n t -> p (w n t)"),
             )
 
-        def normalise(c):
-            shape = [P, PAIRS, P, PACK]
+        def normalise(c, n_half):
+            rows = slice(c * CHUNK * OFFSETS, (c + 1) * CHUNK * OFFSETS)
+            offsets = slice(n_half * N_HALF, (n_half + 1) * N_HALF)
+            shape = [P, CHUNK * OFFSETS, N_HALF, PACK]
             nc.vector.tensor_tensor(
-                out=w_bf[:, c],
-                in0=g[:, c].rearrange("p (t j) n -> p j n t", t=PACK),
-                in1=norms[c][:, SPREAD : SPREAD + PAIRS * P]
-                .rearrange("p (j n) -> p j n", j=PAIRS)
+                out=w_bf[:, c, :, offsets],
+                in0=g[:].rearrange("p t w (m n) -> p (w m) n t", m=OFFSETS)[:, rows, offsets],
+                in1=norms[n_half][:, :, rows]
+                .rearrange("p n r -> p r n")
                 .unsqueeze(3)
+                .to_broadcast(shape),
+                op=ALU.mult,
+            )
+
+        def normalise_last():
+            shape = [P, CHUNK * W_COLS, PACK]
+            nc.vector.tensor_tensor(
+                out=w_bf[:, LAST].rearrange("p r n t -> p (r n) t"),
+                in0=g[:, :, LAST * CHUNK : WINDOWS].rearrange("p t w k -> p (w k) t"),
+                in1=norm_last[:, 1]
+                .rearrange("p j k -> p (j k)")
+                .unsqueeze(2)
                 .to_broadcast(shape),
                 op=ALU.mult,
             )
@@ -200,16 +274,16 @@ def tile_normal_nolayer_s_kernel(
             nc.vector.quantize_mx(
                 out=w_codes[:, c].bitcast(FP8X4),
                 scales=w_scales[:, c],
-                in_=w_bf[:, c].rearrange("p j n t -> p (j n t)"),
+                in_=w_bf[:, c].rearrange("p r n t -> p (r n t)"),
             )
 
         accs = {}
 
         def multiply(c):
-            accs[c] = ps_out.tile([P, PAIRS, BATCH, X_COLS], F32, name="acc")
+            accs[c] = ps_out.tile([P, PAIRS, 2, X_COLS], F32, name="acc")
             for j in range(PAIRS):
-                w_cols = slice(j * P, (j + 1) * P)
-                x_cols = slice(j * BATCH * X_COLS, (j + 1) * BATCH * X_COLS)
+                w_cols = slice(j * 2 * W_COLS, (j + 1) * 2 * W_COLS)
+                x_cols = slice(j * 2 * X_COLS, (j + 1) * 2 * X_COLS)
                 nc.tensor.matmul_mx(
                     out=accs[c][:, j].rearrange("p a n -> p (a n)"),
                     lhsT=w_codes[:, c, w_cols].bitcast(FP8X4),
@@ -220,39 +294,63 @@ def tile_normal_nolayer_s_kernel(
                     stop=True,
                 )
 
+        out_by_window = out.rearrange("a n v m q k -> (a n) (m q) v k")
+
         def store(c, first_half):
             first_half(out=result[0:64, c], in_=accs[c][0:64, :, 0, :])
             nc.scalar.copy(out=result[64:128, c], in_=accs[c][64:128, :, 1, :])
-            for a in range(BATCH):
-                nc.sync.dma_start(
-                    out=out[a, c * PAIRS : (c + 1) * PAIRS].rearrange(
-                        "j v m n k -> (m n) (j v) k"
-                    ),
-                    in_=result[a * 64 : (a + 1) * 64, c].rearrange(
-                        "p j (v k) -> p (j v) k", k=C_LAST
-                    ),
-                )
+            for a in range(2):
+                for j in range(PAIRS):
+                    nc.sync.dma_start(
+                        out=out_by_window[c * CHUNK + 2 * j + a],
+                        in_=result[a * 64 : (a + 1) * 64, c, j].rearrange(
+                            "p (v k) -> p v k", k=C_LAST
+                        ),
+                    )
 
+        distances(0)
+        limit_sigma()
+        distances(1)
+        invert_sigma()
+        square(0)
+        distances(2)
+        find_exp_scale()
+        square(1)
+        distances(3)
+        square(2)
+        gaussians(0)
+        gaussians(1)
+        gaussians(2)
+        square(3)
+        gaussians(3)
+        for t in range(PACK):
+            sum_over_neighbours(t)
+            products(nc.vector, 0, t)
+            products(nc.gpsimd, 1, t)
+        for window in range(V_WINDOWS, WINDOWS):
+            regroup_x(nc.scalar.copy, window)
+        mask_sums()
+        regroup_x(nc.vector.tensor_copy, 0)
+        pick_sums()
+        regroup_x(nc.vector.tensor_copy, 1)
+        invert_sums()
+        quantise_x(0)
         for c in range(CHUNKS):
-            gaussians(c)
-        for c in range(CHUNKS):
-            regroup_x(c)
-        for c in range(CHUNKS):
-            products(c)
-        sums(0)
-        invert(0)
-        spread(0)
-        sums(1)
-        for c in range(CHUNKS):
-            normalise(c)
-            if c + 1 < CHUNKS:
-                invert(c + 1)
-                spread(c + 1)
-            if c + 2 < CHUNKS:
-                sums(c + 2)
-            quantise_x(c)
+            if c < LAST:
+                normalise(c, 0)
+                normalise(c, 1)
+            else:
+                normalise_last()
+            if c == 0:
+                sum_last()
+            if c == 1:
+                pick_last()
+            if c >= 1:
+                quantise_x(c)
+            if c == 1:
+                invert_last()
             quantise_w(c)
             multiply(c)
             if c >= 1:
                 store(c - 1, nc.scalar.copy)
-        store(CHUNKS - 1, nc.vector.tensor_copy)
+        store(LAST, nc.vector.tensor_copy)

@@ -26,7 +26,6 @@ N_HALF = OFFSETS // 2
 MM_WINDOWS = 12
 MM_ROWS = MM_WINDOWS * OFFSETS
 LAST = CHUNKS - 1
-V_WINDOWS = 2
 MIN_SIGMA = 1e-10
 
 FLOPS = 2 * WINDOWS * P * PACK * X_COLS * W_COLS
@@ -157,10 +156,10 @@ def tile_normal_nolayer_s_kernel(
                 scale=exp_scale[:, 0:1],
             )
 
-        def products(engine, half, t):
+        def products(half, t):
             windows = slice(half * HALF, (half + 1) * HALF)
             shape = [P, HALF, OFFSETS, OFFSETS]
-            engine.tensor_tensor(
+            nc.vector.tensor_tensor(
                 out=g[:, t, windows].rearrange("p w (m n) -> p w m n", m=OFFSETS),
                 in0=gauss[:, t, 0, windows].unsqueeze(3).to_broadcast(shape),
                 in1=gauss[:, t, 1, windows].unsqueeze(2).to_broadcast(shape),
@@ -231,8 +230,8 @@ def tile_normal_nolayer_s_kernel(
                     identity=ident_f32[:],
                 )
 
-        def regroup_x(copy, window):
-            copy(
+        def regroup_x(window):
+            nc.scalar.copy(
                 out=x_grouped[:, window].rearrange("p (n i) t -> p n t i", i=4),
                 in_=x_rows[:, window].rearrange("p t (n i) -> p n t i", i=4),
             )
@@ -325,16 +324,16 @@ def tile_normal_nolayer_s_kernel(
         gaussians(3)
         for t in range(PACK):
             sum_over_neighbours(t)
-            products(nc.vector, 0, t)
-            products(nc.gpsimd, 1, t)
-        for window in range(V_WINDOWS, WINDOWS):
-            regroup_x(nc.scalar.copy, window)
+            products(0, t)
+        for window in range(WINDOWS):
+            regroup_x(window)
         mask_sums()
-        regroup_x(nc.vector.tensor_copy, 0)
+        products(1, 0)
         pick_sums()
-        regroup_x(nc.vector.tensor_copy, 1)
+        products(1, 1)
         invert_sums()
-        quantise_x(0)
+        products(1, 2)
+        products(1, 3)
         for c in range(CHUNKS):
             if c < LAST:
                 normalise(c, 0)
@@ -345,8 +344,7 @@ def tile_normal_nolayer_s_kernel(
                 sum_last()
             if c == 1:
                 pick_last()
-            if c >= 1:
-                quantise_x(c)
+            quantise_x(c)
             if c == 1:
                 invert_last()
             quantise_w(c)

@@ -21,11 +21,11 @@ C_LAST = 32
 CHUNK = 4
 CHUNKS = WINDOWS // CHUNK
 PAIRS = CHUNK // 2
+PAIR_COLS = 3 * W_COLS
+W_PLANE = WINDOWS // 2 * PAIR_COLS + W_COLS
 HALF = WINDOWS // 2
-N_HALF = OFFSETS // 2
-MM_WINDOWS = 12
-MM_ROWS = MM_WINDOWS * OFFSETS
 LAST = CHUNKS - 1
+REDUCE_AFTER = (5, 8, 10)
 MIN_SIGMA = 1e-10
 
 FLOPS = 2 * WINDOWS * P * PACK * X_COLS * W_COLS
@@ -46,32 +46,28 @@ def tile_normal_nolayer_s_kernel(
         sigma_bf = keep.tile([P, 1], BF16)
         x_rows = keep.tile([P, WINDOWS, PACK, X_COLS], BF16)
         ident_bf = keep.tile([P, P], BF16)
+        window_order = keep.tile([P, P], BF16)
         ident_f32 = keep.tile([P, P], F32)
-        same_window = keep.tile([P, MM_ROWS], F32)
         ones = keep.tile([P, 1], F32)
         table_warm = keep.tile([P, 1], F32)
         sigma_f32 = keep.tile([P, 1], F32)
         inv_sigma = keep.tile([P, 1], F32)
         exp_scale = keep.tile([P, 1], F32)
-        dist = keep.tile([P, PACK, 2, WINDOWS, OFFSETS], F32)
-        gauss = keep.tile([P, PACK, 2, WINDOWS, OFFSETS], F32)
-        g = keep.tile([P, PACK, WINDOWS, W_COLS], F32)
-        sums_masked = keep.tile([P, MM_WINDOWS, OFFSETS], F32)
-        g_sums = keep.tile([P, OFFSETS], F32)
-        inv_sums = keep.tile([P, OFFSETS], F32)
-        last_sums = keep.tile([P, PAIRS], F32)
-        inv_last = keep.tile([P, PAIRS], F32)
+        dist = keep.tile([P, 2, WINDOWS, OFFSETS, PACK], F32)
+        gauss = keep.tile([P, 2, WINDOWS, OFFSETS, PACK], F32)
+        g = keep.tile([P, WINDOWS, OFFSETS, OFFSETS, PACK], F32)
+        g_sums = keep.tile([P, CHUNKS, PAIRS], F32)
+        summands = keep.tile([P, P], F32)
+        inv_sums = keep.tile([P, CHUNKS, PAIRS], F32)
         x_grouped = keep.tile([P, WINDOWS, X_COLS, PACK], BF16, align_bytes=64)
         x_codes = keep.tile([P, CHUNKS, CHUNK * X_COLS], U32, align_bytes=64)
         x_scales = keep.tile([P, CHUNKS, CHUNK * X_COLS], U8, align_bytes=64)
         w_bf = keep.tile([P, CHUNKS, CHUNK * OFFSETS, OFFSETS, PACK], BF16, align_bytes=64)
-        w_codes = keep.tile([P, CHUNKS, CHUNK * W_COLS], U32, align_bytes=64)
-        w_scales = keep.tile([P, CHUNKS, CHUNK * W_COLS], U8, align_bytes=64)
+        w_codes = keep.tile([P, W_PLANE], U32, align_bytes=64)
+        w_scales = keep.tile([P, W_PLANE], U8, align_bytes=64)
         result = keep.tile([P, CHUNKS, PAIRS, X_COLS], F32)
         coords_t = ps.tile([P, PACK, P], BF16, name="coords_t")
-        cross_sums = ps.tile([P, MM_ROWS], F32, name="cross_sums")
-        norm_last = ps.tile([P, 2, PAIRS, P], F32, name="norm_last")
-        norms = [ps.tile([P, N_HALF, P], F32, name="norm%d" % i) for i in range(2)]
+        norms = [ps.tile([P, 2, PAIRS, P], F32, name="norm%d" % c) for c in range(CHUNKS)]
 
         for w, coords_w in enumerate((coords_lon, coords_lat)):
             nc.sync.dma_start(
@@ -92,36 +88,40 @@ def tile_normal_nolayer_s_kernel(
         nc.vector.memset(coords[2 * WINDOWS : 64, :], 0.0)
         nc.vector.memset(coords[64:P, :], 0.0)
         nc.vector.memset(ones[:], 1.0)
-        nc.vector.memset(inv_sums[MM_ROWS:P, :], 1.0)
-        make_identity(nc, ident_bf[:])
-        make_identity(nc, ident_f32[:])
-        nc.gpsimd.memset(same_window[:], 1.0)
-        for op, base, sign in ((ALU.is_ge, 0, 1), (ALU.is_gt, OFFSETS, -1)):
-            nc.gpsimd.affine_select(
-                out=same_window[:],
-                in_=same_window[:],
-                compare_op=op,
-                fill=0.0,
-                base=base,
-                pattern=[[-sign * OFFSETS, MM_WINDOWS], [0, OFFSETS]],
-                channel_multiplier=sign,
+        for plane in (w_codes, w_scales):
+            nc.vector.memset(
+                plane[:, 0 : W_PLANE - W_COLS].rearrange("p (q k) -> p q k", k=PAIR_COLS)[
+                    :, :, 0:W_COLS
+                ],
+                0,
             )
+            nc.vector.memset(plane[:, W_PLANE - W_COLS : W_PLANE], 0)
+        make_identity(nc, ident_bf[:])
+        nc.gpsimd.tensor_copy(
+            out=window_order[:].rearrange("p (q j h) -> p q j h", j=2, h=2),
+            in_=ident_bf[:].rearrange("p (q h j) -> p q j h", j=2, h=2),
+        )
+        make_identity(nc, ident_f32[:])
         nc.scalar.activation(out=table_warm[:], in_=ones[:], func=ACT.Exp)
 
         for t in range(PACK):
             nc.tensor.transpose(
-                out=coords_t[:, t], in_=coords[:, t::PACK], identity=ident_bf[:]
+                out=coords_t[:, t], in_=coords[:, t::PACK], identity=window_order[:]
             )
 
-        def distances(t):
-            shape = [P, 2, WINDOWS, OFFSETS]
+        def half_of(h):
+            return slice(h * HALF, (h + 1) * HALF)
+
+        def distances(d, h):
+            shape = [P, HALF, OFFSETS, PACK]
+            first = d * WINDOWS + h * HALF
             nc.vector.tensor_tensor(
-                out=dist[:, t],
-                in0=coords_t[:, t, 0 : 2 * WINDOWS]
-                .rearrange("p (d w) -> p d w", d=2)
-                .unsqueeze(3)
+                out=dist[:, d, half_of(h)],
+                in0=coords_t[:, :, first : first + HALF]
+                .rearrange("p t w -> p w t")
+                .unsqueeze(2)
                 .to_broadcast(shape),
-                in1=mus[:, :, 0:OFFSETS].unsqueeze(2).to_broadcast(shape),
+                in1=mus[:, d, 0:OFFSETS].unsqueeze(1).unsqueeze(3).to_broadcast(shape),
                 op=ALU.subtract,
             )
 
@@ -141,92 +141,64 @@ def tile_normal_nolayer_s_kernel(
                 op1=ALU.mult,
             )
 
-        def square(t):
-            flat = dist[:, t].rearrange("p d w m -> p (d w m)")
-            if t == 0:
+        def square(d, h):
+            flat = dist[:, d, half_of(h)].rearrange("p w m t -> p (w m t)")
+            if d == 0:
                 nc.scalar.activation(out=flat, in_=flat, func=ACT.Square)
             else:
                 nc.vector.tensor_tensor(out=flat, in0=flat, in1=flat, op=ALU.mult)
 
-        def gaussians(t):
+        def gaussians(d, h):
             nc.scalar.activation(
-                out=gauss[:, t].rearrange("p d w m -> p (d w m)"),
-                in_=dist[:, t].rearrange("p d w m -> p (d w m)"),
+                out=gauss[:, d, half_of(h)].rearrange("p w m t -> p (w m t)"),
+                in_=dist[:, d, half_of(h)].rearrange("p w m t -> p (w m t)"),
                 func=ACT.Exp,
                 scale=exp_scale[:, 0:1],
             )
 
-        def products(half, t):
-            windows = slice(half * HALF, (half + 1) * HALF)
-            shape = [P, HALF, OFFSETS, OFFSETS]
+        def products(pair):
+            windows = slice(2 * pair, 2 * pair + 2)
+            shape = [P, 2, OFFSETS, OFFSETS, PACK]
             nc.vector.tensor_tensor(
-                out=g[:, t, windows].rearrange("p w (m n) -> p w m n", m=OFFSETS),
-                in0=gauss[:, t, 0, windows].unsqueeze(3).to_broadcast(shape),
-                in1=gauss[:, t, 1, windows].unsqueeze(2).to_broadcast(shape),
+                out=g[:, windows],
+                in0=gauss[:, 0, windows].unsqueeze(3).to_broadcast(shape),
+                in1=gauss[:, 1, windows].unsqueeze(2).to_broadcast(shape),
                 op=ALU.mult,
             )
 
-        def sum_over_neighbours(t):
-            nc.tensor.matmul(
-                out=cross_sums[:],
-                lhsT=gauss[:, t, 0].rearrange("p w m -> p (w m)"),
-                rhs=gauss[:, t, 1, 0:MM_WINDOWS].rearrange("p w m -> p (w m)"),
-                start=(t == 0),
-                stop=(t == PACK - 1),
-            )
-
-        def mask_sums():
-            nc.vector.tensor_tensor(
-                out=sums_masked[0:MM_ROWS].rearrange("p w n -> p (w n)"),
-                in0=cross_sums[0:MM_ROWS],
-                in1=same_window[0:MM_ROWS],
-                op=ALU.mult,
-            )
-
-        def pick_sums():
-            nc.vector.tensor_reduce(
-                out=g_sums[0:MM_ROWS],
-                in_=sums_masked[0:MM_ROWS].rearrange("p w n -> p n w"),
-                axis=mybir.AxisListType.X,
-                op=ALU.add,
-            )
-
-        def invert_sums():
-            nc.vector.reciprocal(out=inv_sums[0:MM_ROWS], in_=g_sums[0:MM_ROWS])
-            for n in range(OFFSETS):
-                nc.tensor.transpose(
-                    out=norms[n // N_HALF][:, n % N_HALF],
-                    in_=inv_sums[:, n : n + 1].to_broadcast([P, P]),
-                    identity=ident_f32[:],
+        def sum_pair(c, j):
+            first = c * CHUNK + 2 * j
+            by_t = g[:, first : first + 2].rearrange("p w m n t -> p (w m n) t")
+            for t in range(PACK):
+                nc.tensor.matmul(
+                    out=norms[c][:, 0, j],
+                    lhsT=by_t[:, :, t],
+                    rhs=ident_f32[:],
+                    is_transpose=True,
+                    start=(t == 0),
+                    stop=(t == PACK - 1),
                 )
 
-        def sum_last():
+        def reduce_sums(c):
+            if c == 0:
+                nc.vector.tensor_reduce(
+                    out=g_sums[:, c], in_=norms[c][:, 0], axis=mybir.AxisListType.X, op=ALU.add
+                )
+                return
             for j in range(PAIRS):
-                first = LAST * CHUNK + 2 * j
-                for t in range(PACK):
-                    nc.tensor.matmul(
-                        out=norm_last[:, 0, j],
-                        lhsT=g[:, t, first : first + 2].rearrange("p w k -> p (w k)"),
-                        rhs=ident_f32[:],
-                        is_transpose=True,
-                        start=(t == 0),
-                        stop=(t == PACK - 1),
-                    )
+                nc.scalar.activation(
+                    out=summands[:],
+                    in_=norms[c][:, 0, j],
+                    func=ACT.Copy,
+                    accum_out=g_sums[:, c, j : j + 1],
+                )
 
-        def pick_last():
-            nc.vector.tensor_reduce(
-                out=last_sums[:],
-                in_=norm_last[:, 0],
-                axis=mybir.AxisListType.X,
-                op=ALU.add,
-            )
-
-        def invert_last():
-            nc.vector.reciprocal(out=inv_last[:], in_=last_sums[:])
+        def invert(c):
+            nc.vector.reciprocal(out=inv_sums[:, c], in_=g_sums[:, c])
             for j in range(PAIRS):
                 nc.tensor.transpose(
-                    out=norm_last[:, 1, j],
-                    in_=inv_last[:, j : j + 1].to_broadcast([P, P]),
+                    out=norms[c][:, 1, j],
+                    in_=inv_sums[:, c, j : j + 1].to_broadcast([P, P]),
                     identity=ident_f32[:],
                 )
 
@@ -243,112 +215,108 @@ def tile_normal_nolayer_s_kernel(
                 in_=x_grouped[:, c * CHUNK : (c + 1) * CHUNK].rearrange("p w n t -> p (w n t)"),
             )
 
-        def normalise(c, n_half):
-            rows = slice(c * CHUNK * OFFSETS, (c + 1) * CHUNK * OFFSETS)
-            offsets = slice(n_half * N_HALF, (n_half + 1) * N_HALF)
-            shape = [P, CHUNK * OFFSETS, N_HALF, PACK]
-            nc.vector.tensor_tensor(
-                out=w_bf[:, c, :, offsets],
-                in0=g[:].rearrange("p t w (m n) -> p (w m) n t", m=OFFSETS)[:, rows, offsets],
-                in1=norms[n_half][:, :, rows]
-                .rearrange("p n r -> p r n")
-                .unsqueeze(3)
-                .to_broadcast(shape),
-                op=ALU.mult,
-            )
-
-        def normalise_last():
+        def normalise(c):
             shape = [P, CHUNK * W_COLS, PACK]
             nc.vector.tensor_tensor(
-                out=w_bf[:, LAST].rearrange("p r n t -> p (r n) t"),
-                in0=g[:, :, LAST * CHUNK : WINDOWS].rearrange("p t w k -> p (w k) t"),
-                in1=norm_last[:, 1]
+                out=w_bf[:, c].rearrange("p r n t -> p (r n) t"),
+                in0=g[:, c * CHUNK : (c + 1) * CHUNK].rearrange("p w m n t -> p (w m n) t"),
+                in1=norms[c][:, 1]
                 .rearrange("p j k -> p (j k)")
                 .unsqueeze(2)
                 .to_broadcast(shape),
                 op=ALU.mult,
             )
 
-        def quantise_w(c):
+        def quantise_w(c, j):
+            start = (c * PAIRS + j) * PAIR_COLS + W_COLS
+            cols = slice(start, start + 2 * W_COLS)
+            rows = slice(j * 2 * OFFSETS, (j + 1) * 2 * OFFSETS)
             nc.vector.quantize_mx(
-                out=w_codes[:, c].bitcast(FP8X4),
-                scales=w_scales[:, c],
-                in_=w_bf[:, c].rearrange("p r n t -> p (r n t)"),
+                out=w_codes[:, cols].bitcast(FP8X4),
+                scales=w_scales[:, cols],
+                in_=w_bf[:, c, rows].rearrange("p r n t -> p (r n t)"),
             )
 
         accs = {}
 
-        def multiply(c):
-            accs[c] = ps_out.tile([P, PAIRS, 2, X_COLS], F32, name="acc")
-            for j in range(PAIRS):
-                w_cols = slice(j * 2 * W_COLS, (j + 1) * 2 * W_COLS)
-                x_cols = slice(j * 2 * X_COLS, (j + 1) * 2 * X_COLS)
+        def multiply(c, j):
+            if j == 0 or c == LAST:
+                accs[c, j] = ps_out.tile([P, PAIRS, X_COLS], F32, name="acc")
+            acc = accs[c, j] if c == LAST else accs[c, 0]
+            slot = 0 if c == LAST else j
+            for a in range(2):
+                start = (c * PAIRS + j) * PAIR_COLS + 2 * a * W_COLS
+                w_cols = slice(start, start + 2 * W_COLS)
+                x_cols = slice((2 * a + j) * X_COLS, (2 * a + j + 1) * X_COLS)
                 nc.tensor.matmul_mx(
-                    out=accs[c][:, j].rearrange("p a n -> p (a n)"),
-                    lhsT=w_codes[:, c, w_cols].bitcast(FP8X4),
-                    lhsT_scale=w_scales[:, c, w_cols],
+                    out=acc[:, slot],
+                    lhsT=w_codes[:, w_cols].bitcast(FP8X4),
+                    lhsT_scale=w_scales[:, w_cols],
                     rhs=x_codes[:, c, x_cols].bitcast(FP8X4),
                     rhs_scale=x_scales[:, c, x_cols],
-                    start=True,
-                    stop=True,
+                    start=(a == 0),
+                    stop=(a == 1),
                 )
 
-        out_by_window = out.rearrange("a n v m q k -> (a n) (m q) v k")
+        out_by_window = out.rearrange("a n v m q k -> (a n) v (m q) k")
 
-        def store(c, first_half):
-            first_half(out=result[0:64, c], in_=accs[c][0:64, :, 0, :])
-            nc.scalar.copy(out=result[64:128, c], in_=accs[c][64:128, :, 1, :])
+        def store_rows(c, a, queue):
+            first = c * CHUNK + 2 * a
+            queue.dma_start(
+                out=out_by_window[first : first + 2].rearrange("j v q k -> q (j v) k"),
+                in_=result[(1 - a) * 64 : (2 - a) * 64, c].rearrange(
+                    "p j (v k) -> p (j v) k", k=C_LAST
+                ),
+            )
+
+        def store(c):
+            nc.scalar.copy(out=result[:, c], in_=accs[c, 0][:])
             for a in range(2):
-                for j in range(PAIRS):
-                    nc.sync.dma_start(
-                        out=out_by_window[c * CHUNK + 2 * j + a],
-                        in_=result[a * 64 : (a + 1) * 64, c, j].rearrange(
-                            "p (v k) -> p v k", k=C_LAST
-                        ),
-                    )
+                store_rows(c, a, nc.sync)
 
-        distances(0)
+        distances(0, 0)
         limit_sigma()
-        distances(1)
+        distances(1, 0)
         invert_sigma()
-        square(0)
-        distances(2)
+        square(0, 0)
+        square(1, 0)
         find_exp_scale()
-        square(1)
-        distances(3)
-        square(2)
-        gaussians(0)
-        gaussians(1)
-        gaussians(2)
-        square(3)
-        gaussians(3)
-        for t in range(PACK):
-            sum_over_neighbours(t)
-            products(0, t)
+        distances(0, 1)
+        distances(1, 1)
+        gaussians(0, 0)
+        gaussians(1, 0)
+        square(0, 1)
+        square(1, 1)
+        gaussians(0, 1)
+        gaussians(1, 1)
+        for pair in range(CHUNKS * PAIRS):
+            products(pair)
+            if pair == 3:
+                reduce_sums(0)
+            if pair == 4:
+                invert(0)
+            sum_pair(pair // PAIRS, pair % PAIRS)
         for window in range(WINDOWS):
             regroup_x(window)
-        mask_sums()
-        products(1, 0)
-        pick_sums()
-        products(1, 1)
-        invert_sums()
-        products(1, 2)
-        products(1, 3)
-        for c in range(CHUNKS):
+            if window in REDUCE_AFTER:
+                reduce_sums(REDUCE_AFTER.index(window) + 1)
+        normalise(0)
+        invert(1)
+        quantise_x(0)
+        quantise_w(0, 0)
+        quantise_w(0, 1)
+        multiply(0, 0)
+        multiply(0, 1)
+        for c in range(1, CHUNKS):
+            normalise(c)
             if c < LAST:
-                normalise(c, 0)
-                normalise(c, 1)
-            else:
-                normalise_last()
-            if c == 0:
-                sum_last()
-            if c == 1:
-                pick_last()
+                invert(c + 1)
             quantise_x(c)
-            if c == 1:
-                invert_last()
-            quantise_w(c)
-            multiply(c)
-            if c >= 1:
-                store(c - 1, nc.scalar.copy)
-        store(LAST, nc.vector.tensor_copy)
+            for j in range(PAIRS):
+                quantise_w(c, j)
+                multiply(c, j)
+            store(c - 1)
+        nc.vector.tensor_copy(out=result[:, LAST, 0], in_=accs[LAST, 0][:, 0])
+        nc.scalar.copy(out=result[:, LAST, 1], in_=accs[LAST, 1][:, 0])
+        store_rows(LAST, 0, nc.sync)
+        store_rows(LAST, 1, nc.scalar)

@@ -25,7 +25,8 @@ PAIR_COLS = 3 * W_COLS
 W_PLANE = WINDOWS // 2 * PAIR_COLS + W_COLS
 HALF = WINDOWS // 2
 LAST = CHUNKS - 1
-REDUCE_AFTER = (5, 8, 10)
+V_WINDOWS = 2
+REDUCE_AFTER = (7, 9, 11)
 MIN_SIGMA = 1e-10
 
 FLOPS = 2 * WINDOWS * P * PACK * X_COLS * W_COLS
@@ -143,10 +144,7 @@ def tile_normal_nolayer_s_kernel(
 
         def square(d, h):
             flat = dist[:, d, half_of(h)].rearrange("p w m t -> p (w m t)")
-            if d == 0:
-                nc.scalar.activation(out=flat, in_=flat, func=ACT.Square)
-            else:
-                nc.vector.tensor_tensor(out=flat, in0=flat, in1=flat, op=ALU.mult)
+            nc.scalar.activation(out=flat, in_=flat, func=ACT.Square)
 
         def gaussians(d, h):
             nc.scalar.activation(
@@ -202,8 +200,8 @@ def tile_normal_nolayer_s_kernel(
                     identity=ident_f32[:],
                 )
 
-        def regroup_x(window):
-            nc.scalar.copy(
+        def regroup_x(copy, window):
+            copy(
                 out=x_grouped[:, window].rearrange("p (n i) t -> p n t i", i=4),
                 in_=x_rows[:, window].rearrange("p t (n i) -> p n t i", i=4),
             )
@@ -278,17 +276,16 @@ def tile_normal_nolayer_s_kernel(
         limit_sigma()
         distances(1, 0)
         invert_sigma()
-        square(0, 0)
-        square(1, 0)
-        find_exp_scale()
         distances(0, 1)
+        find_exp_scale()
         distances(1, 1)
-        gaussians(0, 0)
-        gaussians(1, 0)
-        square(0, 1)
-        square(1, 1)
-        gaussians(0, 1)
-        gaussians(1, 1)
+        for h in range(2):
+            for d in range(2):
+                square(d, h)
+            for d in range(2):
+                gaussians(d, h)
+        for window in range(V_WINDOWS):
+            regroup_x(nc.vector.tensor_copy, window)
         for pair in range(CHUNKS * PAIRS):
             products(pair)
             if pair == 3:
@@ -296,8 +293,8 @@ def tile_normal_nolayer_s_kernel(
             if pair == 4:
                 invert(0)
             sum_pair(pair // PAIRS, pair % PAIRS)
-        for window in range(WINDOWS):
-            regroup_x(window)
+        for window in range(V_WINDOWS, WINDOWS):
+            regroup_x(nc.scalar.copy, window)
             if window in REDUCE_AFTER:
                 reduce_sums(REDUCE_AFTER.index(window) + 1)
         normalise(0)

@@ -26,7 +26,7 @@ W_PLANE = WINDOWS // 2 * PAIR_COLS + W_COLS
 HALF = WINDOWS // 2
 LAST = CHUNKS - 1
 V_WINDOWS = 2
-REDUCE_AFTER = (7, 9, 11)
+REDUCE_AFTER = (8, 11, 14)
 MIN_SIGMA = 1e-10
 
 FLOPS = 2 * WINDOWS * P * PACK * X_COLS * W_COLS

from contextlib import ExitStack

import concourse.mybir as mybir
from concourse.masks import make_identity

F32 = mybir.dt.float32
BF16 = mybir.dt.bfloat16
U32 = mybir.dt.uint32
U8 = mybir.dt.uint8
FP8X4 = mybir.dt.float8_e4m3fn_x4
ACT = mybir.ActivationFunctionType
ALU = mybir.AluOpType

P = 128
PACK = 4
WINDOWS = 16
OFFSETS = 8
W_COLS = OFFSETS * OFFSETS
X_COLS = 128
C_LAST = 32
CHUNK = 4
CHUNKS = WINDOWS // CHUNK
PAIRS = CHUNK // 2
PAIR_COLS = 3 * W_COLS
W_PLANE = WINDOWS // 2 * PAIR_COLS + W_COLS
HALF = WINDOWS // 2
LAST = CHUNKS - 1
V_WINDOWS = 2
REDUCE_AFTER = (8, 11, 14)
MIN_SIGMA = 1e-10

FLOPS = 2 * WINDOWS * P * PACK * X_COLS * W_COLS


def tile_normal_nolayer_s_kernel(
    tc, x, coords_lon, coords_lat, mus_lon, mus_lat, sigma, out
):
    nc = tc.nc
    with ExitStack() as ctx:
        keep = ctx.enter_context(tc.tile_pool(name="keep", bufs=1))
        ps = ctx.enter_context(tc.psum_pool(name="ps", bufs=1))
        ps_out = ctx.enter_context(tc.psum_pool(name="ps_out", bufs=3))
        ctx.enter_context(tc.manual_schedule())

        coords = keep.tile([P, P * PACK], BF16)
        mus = keep.tile([P, 2, 16], BF16)
        sigma_bf = keep.tile([P, 1], BF16)
        x_rows = keep.tile([P, WINDOWS, PACK, X_COLS], BF16)
        ident_bf = keep.tile([P, P], BF16)
        window_order = keep.tile([P, P], BF16)
        ident_f32 = keep.tile([P, P], F32)
        ones = keep.tile([P, 1], F32)
        table_warm = keep.tile([P, 1], F32)
        sigma_f32 = keep.tile([P, 1], F32)
        inv_sigma = keep.tile([P, 1], F32)
        exp_scale = keep.tile([P, 1], F32)
        dist = keep.tile([P, 2, WINDOWS, OFFSETS, PACK], F32)
        gauss = keep.tile([P, 2, WINDOWS, OFFSETS, PACK], F32)
        g = keep.tile([P, WINDOWS, OFFSETS, OFFSETS, PACK], F32)
        g_sums = keep.tile([P, CHUNKS, PAIRS], F32)
        summands = keep.tile([P, P], F32)
        inv_sums = keep.tile([P, CHUNKS, PAIRS], F32)
        x_grouped = keep.tile([P, WINDOWS, X_COLS, PACK], BF16, align_bytes=64)
        x_codes = keep.tile([P, CHUNKS, CHUNK * X_COLS], U32, align_bytes=64)
        x_scales = keep.tile([P, CHUNKS, CHUNK * X_COLS], U8, align_bytes=64)
        w_bf = keep.tile([P, CHUNKS, CHUNK * OFFSETS, OFFSETS, PACK], BF16, align_bytes=64)
        w_codes = keep.tile([P, W_PLANE], U32, align_bytes=64)
        w_scales = keep.tile([P, W_PLANE], U8, align_bytes=64)
        result = keep.tile([P, CHUNKS, PAIRS, X_COLS], F32)
        coords_t = ps.tile([P, PACK, P], BF16, name="coords_t")
        norms = [ps.tile([P, 2, PAIRS, P], F32, name="norm%d" % c) for c in range(CHUNKS)]

        for w, coords_w in enumerate((coords_lon, coords_lat)):
            nc.sync.dma_start(
                out=coords[w * WINDOWS : (w + 1) * WINDOWS, :],
                in_=coords_w.rearrange("a n o i h -> (a n o) (i h)"),
            )
        nc.scalar.dma_start(out=mus[:, 0, 0:OFFSETS], in_=mus_lon.partition_broadcast(P))
        nc.sync.dma_start(out=mus[:, 1, 0:OFFSETS], in_=mus_lat.partition_broadcast(P))
        nc.scalar.dma_start(out=sigma_bf[:], in_=sigma.partition_broadcast(P))
        x_by_window = x.rearrange("a n o (p t) v k -> p (a n o) (t v k)", t=PACK)
        for c in range(CHUNKS):
            windows = slice(c * CHUNK, (c + 1) * CHUNK)
            nc.sync.dma_start(
                out=x_rows[:, windows].rearrange("p w t n -> p w (t n)"),
                in_=x_by_window[:, windows],
            )

        nc.vector.memset(coords[2 * WINDOWS : 64, :], 0.0)
        nc.vector.memset(coords[64:P, :], 0.0)
        nc.vector.memset(ones[:], 1.0)
        for plane in (w_codes, w_scales):
            nc.vector.memset(
                plane[:, 0 : W_PLANE - W_COLS].rearrange("p (q k) -> p q k", k=PAIR_COLS)[
                    :, :, 0:W_COLS
                ],
                0,
            )
            nc.vector.memset(plane[:, W_PLANE - W_COLS : W_PLANE], 0)
        make_identity(nc, ident_bf[:])
        nc.gpsimd.tensor_copy(
            out=window_order[:].rearrange("p (q j h) -> p q j h", j=2, h=2),
            in_=ident_bf[:].rearrange("p (q h j) -> p q j h", j=2, h=2),
        )
        make_identity(nc, ident_f32[:])
        nc.scalar.activation(out=table_warm[:], in_=ones[:], func=ACT.Exp)

        for t in range(PACK):
            nc.tensor.transpose(
                out=coords_t[:, t], in_=coords[:, t::PACK], identity=window_order[:]
            )

        def half_of(h):
            return slice(h * HALF, (h + 1) * HALF)

        def distances(d, h):
            shape = [P, HALF, OFFSETS, PACK]
            first = d * WINDOWS + h * HALF
            nc.vector.tensor_tensor(
                out=dist[:, d, half_of(h)],
                in0=coords_t[:, :, first : first + HALF]
                .rearrange("p t w -> p w t")
                .unsqueeze(2)
                .to_broadcast(shape),
                in1=mus[:, d, 0:OFFSETS].unsqueeze(1).unsqueeze(3).to_broadcast(shape),
                op=ALU.subtract,
            )

        def limit_sigma():
            nc.vector.tensor_scalar_max(out=sigma_f32[:], in0=sigma_bf[:], scalar1=MIN_SIGMA)

        def invert_sigma():
            nc.vector.reciprocal(out=inv_sigma[:], in_=sigma_f32[:])

        def find_exp_scale():
            nc.vector.scalar_tensor_tensor(
                out=exp_scale[:],
                in0=inv_sigma[:],
                scalar=-0.5,
                in1=inv_sigma[:],
                op0=ALU.mult,
                op1=ALU.mult,
            )

        def square(d, h):
            flat = dist[:, d, half_of(h)].rearrange("p w m t -> p (w m t)")
            nc.scalar.activation(out=flat, in_=flat, func=ACT.Square)

        def gaussians(d, h):
            nc.scalar.activation(
                out=gauss[:, d, half_of(h)].rearrange("p w m t -> p (w m t)"),
                in_=dist[:, d, half_of(h)].rearrange("p w m t -> p (w m t)"),
                func=ACT.Exp,
                scale=exp_scale[:, 0:1],
            )

        def products(pair):
            windows = slice(2 * pair, 2 * pair + 2)
            shape = [P, 2, OFFSETS, OFFSETS, PACK]
            nc.vector.tensor_tensor(
                out=g[:, windows],
                in0=gauss[:, 0, windows].unsqueeze(3).to_broadcast(shape),
                in1=gauss[:, 1, windows].unsqueeze(2).to_broadcast(shape),
                op=ALU.mult,
            )

        def sum_pair(c, j):
            first = c * CHUNK + 2 * j
            by_t = g[:, first : first + 2].rearrange("p w m n t -> p (w m n) t")
            for t in range(PACK):
                nc.tensor.matmul(
                    out=norms[c][:, 0, j],
                    lhsT=by_t[:, :, t],
                    rhs=ident_f32[:],
                    is_transpose=True,
                    start=(t == 0),
                    stop=(t == PACK - 1),
                )

        def reduce_sums(c):
            if c == 0:
                nc.vector.tensor_reduce(
                    out=g_sums[:, c], in_=norms[c][:, 0], axis=mybir.AxisListType.X, op=ALU.add
                )
                return
            for j in range(PAIRS):
                nc.scalar.activation(
                    out=summands[:],
                    in_=norms[c][:, 0, j],
                    func=ACT.Copy,
                    accum_out=g_sums[:, c, j : j + 1],
                )

        def invert(c):
            nc.vector.reciprocal(out=inv_sums[:, c], in_=g_sums[:, c])
            for j in range(PAIRS):
                nc.tensor.transpose(
                    out=norms[c][:, 1, j],
                    in_=inv_sums[:, c, j : j + 1].to_broadcast([P, P]),
                    identity=ident_f32[:],
                )

        def regroup_x(copy, window):
            copy(
                out=x_grouped[:, window].rearrange("p (n i) t -> p n t i", i=4),
                in_=x_rows[:, window].rearrange("p t (n i) -> p n t i", i=4),
            )

        def quantise_x(c):
            nc.vector.quantize_mx(
                out=x_codes[:, c].bitcast(FP8X4),
                scales=x_scales[:, c],
                in_=x_grouped[:, c * CHUNK : (c + 1) * CHUNK].rearrange("p w n t -> p (w n t)"),
            )

        def normalise(c):
            shape = [P, CHUNK * W_COLS, PACK]
            nc.vector.tensor_tensor(
                out=w_bf[:, c].rearrange("p r n t -> p (r n) t"),
                in0=g[:, c * CHUNK : (c + 1) * CHUNK].rearrange("p w m n t -> p (w m n) t"),
                in1=norms[c][:, 1]
                .rearrange("p j k -> p (j k)")
                .unsqueeze(2)
                .to_broadcast(shape),
                op=ALU.mult,
            )

        def quantise_w(c, j):
            start = (c * PAIRS + j) * PAIR_COLS + W_COLS
            cols = slice(start, start + 2 * W_COLS)
            rows = slice(j * 2 * OFFSETS, (j + 1) * 2 * OFFSETS)
            nc.vector.quantize_mx(
                out=w_codes[:, cols].bitcast(FP8X4),
                scales=w_scales[:, cols],
                in_=w_bf[:, c, rows].rearrange("p r n t -> p (r n t)"),
            )

        accs = {}

        def multiply(c, j):
            if j == 0 or c == LAST:
                accs[c, j] = ps_out.tile([P, PAIRS, X_COLS], F32, name="acc")
            acc = accs[c, j] if c == LAST else accs[c, 0]
            slot = 0 if c == LAST else j
            for a in range(2):
                start = (c * PAIRS + j) * PAIR_COLS + 2 * a * W_COLS
                w_cols = slice(start, start + 2 * W_COLS)
                x_cols = slice((2 * a + j) * X_COLS, (2 * a + j + 1) * X_COLS)
                nc.tensor.matmul_mx(
                    out=acc[:, slot],
                    lhsT=w_codes[:, w_cols].bitcast(FP8X4),
                    lhsT_scale=w_scales[:, w_cols],
                    rhs=x_codes[:, c, x_cols].bitcast(FP8X4),
                    rhs_scale=x_scales[:, c, x_cols],
                    start=(a == 0),
                    stop=(a == 1),
                )

        out_by_window = out.rearrange("a n v m q k -> (a n) v (m q) k")

        def store_rows(c, a, queue):
            first = c * CHUNK + 2 * a
            queue.dma_start(
                out=out_by_window[first : first + 2].rearrange("j v q k -> q (j v) k"),
                in_=result[(1 - a) * 64 : (2 - a) * 64, c].rearrange(
                    "p j (v k) -> p (j v) k", k=C_LAST
                ),
            )

        def store(c):
            nc.scalar.copy(out=result[:, c], in_=accs[c, 0][:])
            for a in range(2):
                store_rows(c, a, nc.sync)

        distances(0, 0)
        limit_sigma()
        distances(1, 0)
        invert_sigma()
        distances(0, 1)
        find_exp_scale()
        distances(1, 1)
        for h in range(2):
            for d in range(2):
                square(d, h)
            for d in range(2):
                gaussians(d, h)
        for window in range(V_WINDOWS):
            regroup_x(nc.vector.tensor_copy, window)
        for pair in range(CHUNKS * PAIRS):
            products(pair)
            if pair == 3:
                reduce_sums(0)
            if pair == 4:
                invert(0)
            sum_pair(pair // PAIRS, pair % PAIRS)
        for window in range(V_WINDOWS, WINDOWS):
            regroup_x(nc.scalar.copy, window)
            if window in REDUCE_AFTER:
                reduce_sums(REDUCE_AFTER.index(window) + 1)
        normalise(0)
        invert(1)
        quantise_x(0)
        quantise_w(0, 0)
        quantise_w(0, 1)
        multiply(0, 0)
        multiply(0, 1)
        for c in range(1, CHUNKS):
            normalise(c)
            if c < LAST:
                invert(c + 1)
            quantise_x(c)
            for j in range(PAIRS):
                quantise_w(c, j)
                multiply(c, j)
            store(c - 1)
        nc.vector.tensor_copy(out=result[:, LAST, 0], in_=accs[LAST, 0][:, 0])
        nc.scalar.copy(out=result[:, LAST, 1], in_=accs[LAST, 1][:, 0])
        store_rows(LAST, 0, nc.sync)
        store_rows(LAST, 1, nc.scalar)
